import numpy as np
import ml_dtypes


def mxq(x, axis, fmt="e4m3"):
    dtype, down = {"e4m3": (ml_dtypes.float8_e4m3fn, 7), "e5m2": (ml_dtypes.float8_e5m2, 14)}[fmt]
    v = np.moveaxis(np.asarray(x, np.float32).astype(ml_dtypes.bfloat16).astype(np.float64), axis, -1)
    blocks = v.reshape(v.shape[:-1] + (-1, 32))
    amax = np.abs(blocks).max(-1, keepdims=True)
    byte = np.maximum(np.where(amax > 0, np.frexp(amax)[1] - 1 + 127, 0) - down, 1)
    scale = np.exp2(byte - 127.0)
    codes = (blocks / scale).astype(np.float32).astype(dtype).astype(np.float64)
    return np.moveaxis((codes * scale).reshape(v.shape), -1, axis)


WIDE = False


def mx_kscale(k):
    if not WIDE:
        return np.ones(k)
    levels = np.array([20, -20, 10, -10, 0])
    a = np.random.permutation(np.resize(levels, k // 512 * 4)).reshape(k // 512, 4)
    idx = np.arange(k)
    return np.exp2(a[idx // 512, idx % 128 // 32])


BF16 = ml_dtypes.bfloat16


def bf(x):
    return np.asarray(x, np.float32).astype(BF16)


def f64(x):
    return np.asarray(x).astype(np.float64)


B, S, DI, DO = 2, 2048, 1024, 512
Q_LEVELS = 127.0
CX, CW, CO = 127.0 / 8.0, 127.0 / 256.0, 127.0 / 8.0


def on_grid(v, cmax):
    step = cmax / Q_LEVELS
    return np.clip(np.round(v / step), -Q_LEVELS, Q_LEVELS) * step


def setup_inputs():
    u = mx_kscale(DO)
    x = on_grid(np.random.standard_normal((B, S, DI)), CX)
    w = on_grid(np.random.standard_normal((DO, DI)) / np.sqrt(DI), CW) / u[:, None]
    b = np.random.standard_normal(DO) * 0.5
    g = np.random.standard_normal((B, S, DO)) * np.exp2(np.random.randint(-12, 1, (B, S, 1))) * 32.0 * u
    return {"inputs": bf(x), "weight": bf(w), "bias": bf(b),
            "clip_max": bf(np.array([CX, CW, CO])), "grad_out": bf(g)}


def reference(inputs, weight, bias, clip_max, grad_out):
    g = mxq(f64(grad_out), 2, "e5m2")
    w = mxq(f64(weight), 0, "e4m3")
    return g @ w

@@ -1,0 +1,137 @@
+from contextlib import ExitStack
+
+import concourse.mybir as mybir
+from concourse.masks import make_identity
+
+F32 = mybir.dt.float32
+BF16 = mybir.dt.bfloat16
+U32 = mybir.dt.uint32
+U8 = mybir.dt.uint8
+E5M2X4 = mybir.dt.float8_e5m2_x4
+E4M3X4 = mybir.dt.float8_e4m3fn_x4
+
+P = 128
+TOKENS = 4096
+K = 512
+N = 1024
+HALF = 512
+N_TILES = TOKENS // P
+GROUP = 4
+N_GROUPS = N_TILES // GROUP
+LOAD_CHUNKS = ((0, 4), (4, 4), (8, 8), (16, 16))
+STORE_TILES = 2
+
+FLOPS = 2 * TOKENS * K * N
+BYTES = TOKENS * K * 2 + K * N * 2 + TOKENS * N * 4
+
+
+def tile_lsquantlinearlayer_t_kernel(tc, inputs, weight, bias, clip_max, grad_out, out):
+    nc = tc.nc
+    g_rows = grad_out.flatten_outer_dims().rearrange("(p t) k -> p (t k)", t=N_TILES)
+    out_rows = out.flatten_outer_dims().rearrange("(p t) i -> p (t i)", t=N_TILES)
+    w_rows = weight.rearrange("(u q e) c -> q u e c", u=2, e=2)
+
+    with ExitStack() as ctx:
+        keep = ctx.enter_context(tc.tile_pool(name="keep", bufs=1))
+        stage = ctx.enter_context(tc.tile_pool(name="stage", bufs=3))
+        psum_t = ctx.enter_context(tc.psum_pool(name="psum_t", bufs=2))
+        psum_o = ctx.enter_context(tc.psum_pool(name="psum_o", bufs=6))
+        ctx.enter_context(tc.manual_schedule())
+
+        g_words = {}
+        w_raw = keep.tile([P, 4, N], BF16, name="w_raw")
+        for c, (first, count) in enumerate(LOAD_CHUNKS):
+            g_sb = keep.tile([P, count * K], BF16, name="g_sb%d" % c)
+            nc.sync.dma_start(out=g_sb[:], in_=g_rows[:, first * K : (first + count) * K])
+            words = g_sb[:].bitcast(F32)
+            for i in range(count):
+                g_words[first + i] = words[:, i * (K // 2) : (i + 1) * (K // 2)]
+            if c == 0:
+                nc.sync.dma_start(out=w_raw[:].rearrange("p (u e) c -> p u e c", u=2), in_=w_rows)
+
+        ident = keep.tile([P, P], F32, name="ident")
+        make_identity(nc, ident[:])
+
+        def transposes(q):
+            banks = []
+            for b in range(2):
+                tp = psum_t.tile([P, 2, 2, P], F32, name="tp")
+                for a in range(2):
+                    words = g_words[GROUP * q + 2 * b + a]
+                    for u in range(2):
+                        nc.tensor.transpose(tp[:, a, u, :], words[:, u * P : (u + 1) * P], ident[:])
+                banks.append(tp)
+            grouped = stage.tile([P, GROUP * K], BF16, name="grouped", align_bytes=64)
+            pairs = grouped[:].bitcast(F32).rearrange("p (a r u) -> p a r u", a=GROUP, u=2)
+            for b in range(2):
+                nc.scalar.copy(
+                    out=pairs[:, 2 * b : 2 * b + 2, :, :],
+                    in_=banks[b][:].rearrange("p a u r -> p a r u"),
+                )
+            return grouped
+
+        def quantise(grouped):
+            codes = stage.tile([P, GROUP * P], U32, name="g_codes", align_bytes=64)
+            scales = stage.tile([P, GROUP * P], U8, name="g_scales", align_bytes=64)
+            nc.vector.quantize_mx(out=codes[:].bitcast(E5M2X4), scales=scales[:], in_=grouped[:])
+            return codes, scales
+
+        grouped_of = {0: transposes(0)}
+        quantised_of = {0: quantise(grouped_of[0])}
+
+        w_grouped = []
+        for h in range(2):
+            wg = keep.tile([P, HALF, 4], BF16, name="w_grouped%d" % h, align_bytes=64)
+            dst = wg[:].rearrange("p (c i) t -> p c t i", i=4)
+            src = w_raw[:, :, h * HALF : (h + 1) * HALF].rearrange("p t (c i) -> p c t i", i=4)
+            if h == 0:
+                nc.vector.tensor_copy(out=dst, in_=src)
+            else:
+                nc.scalar.copy(out=dst, in_=src)
+            w_grouped.append(wg)
+        w_codes = []
+        w_scales = []
+        for h in range(2):
+            wc = keep.tile([P, HALF], U32, name="w_codes%d" % h, align_bytes=64)
+            ws = keep.tile([P, HALF], U8, name="w_scales%d" % h, align_bytes=64)
+            nc.vector.quantize_mx(
+                out=wc[:].bitcast(E4M3X4),
+                scales=ws[:],
+                in_=w_grouped[h][:].rearrange("p c t -> p (c t)"),
+            )
+            w_codes.append(wc)
+            w_scales.append(ws)
+
+        grouped_of[1] = transposes(1)
+
+        out_sb = None
+        for q in range(N_GROUPS):
+            codes, scales = quantised_of[q]
+            for a in range(GROUP):
+                t = GROUP * q + a
+                if t % STORE_TILES == 0:
+                    out_sb = keep.tile([P, STORE_TILES * N], F32, name="out_sb%d" % t)
+                base = (t % STORE_TILES) * N
+                for h in range(2):
+                    acc = psum_o.tile([P, HALF], F32, name="acc")
+                    nc.tensor.matmul_mx(
+                        out=acc[:],
+                        lhsT=codes[:, a * P : (a + 1) * P].bitcast(E5M2X4),
+                        lhsT_scale=scales[:, a * P : (a + 1) * P],
+                        rhs=w_codes[h][:].bitcast(E4M3X4),
+                        rhs_scale=w_scales[h][:],
+                        start=True,
+                        stop=True,
+                    )
+                    dst = out_sb[:, base + h * HALF : base + (h + 1) * HALF]
+                    if h == 0:
+                        nc.scalar.copy(out=dst, in_=acc[:])
+                    else:
+                        nc.vector.tensor_copy(out=dst, in_=acc[:])
+                if t % STORE_TILES == STORE_TILES - 1:
+                    first = t - STORE_TILES + 1
+                    nc.sync.dma_start(out=out_rows[:, first * N : (t + 1) * N], in_=out_sb[:])
+                if a == 1 and q + 1 < N_GROUPS:
+                    quantised_of[q + 1] = quantise(grouped_of[q + 1])
+            if q + 2 < N_GROUPS:
+                grouped_of[q + 2] = transposes(q + 2)

@@ -17,8 +17,8 @@ N = 1024
 HALF = 512
 N_TILES = TOKENS // P
 GROUP = 4
-N_GROUPS = N_TILES // GROUP
-LOAD_CHUNKS = ((0, 4), (4, 4), (8, 8), (16, 16))
+GROUPS = ((0, 2), (2, 2), (4, 4), (8, 4), (12, 4), (16, 4), (20, 4), (24, 4), (28, 4))
+LOAD_CHUNKS = ((0, 2), (2, 2), (4, 4), (8, 8), (16, 16))
 STORE_TILES = 2
 
 FLOPS = 2 * TOKENS * K * N
@@ -52,32 +52,38 @@ def tile_lsquantlinearlayer_t_kernel(tc, inputs, weight, bias, clip_max, grad_ou
         ident = keep.tile([P, P], F32, name="ident")
         make_identity(nc, ident[:])
 
-        def transposes(q):
+        def transposes(gi):
+            first, count = GROUPS[gi]
             banks = []
-            for b in range(2):
+            for b in range(count // 2):
                 tp = psum_t.tile([P, 2, 2, P], F32, name="tp")
                 for a in range(2):
-                    words = g_words[GROUP * q + 2 * b + a]
+                    words = g_words[first + 2 * b + a]
                     for u in range(2):
                         nc.tensor.transpose(tp[:, a, u, :], words[:, u * P : (u + 1) * P], ident[:])
                 banks.append(tp)
             grouped = stage.tile([P, GROUP * K], BF16, name="grouped", align_bytes=64)
             pairs = grouped[:].bitcast(F32).rearrange("p (a r u) -> p a r u", a=GROUP, u=2)
-            for b in range(2):
+            for b in range(count // 2):
                 nc.scalar.copy(
                     out=pairs[:, 2 * b : 2 * b + 2, :, :],
                     in_=banks[b][:].rearrange("p a u r -> p a r u"),
                 )
             return grouped
 
-        def quantise(grouped):
+        def quantise(gi, grouped):
+            count = GROUPS[gi][1]
             codes = stage.tile([P, GROUP * P], U32, name="g_codes", align_bytes=64)
             scales = stage.tile([P, GROUP * P], U8, name="g_scales", align_bytes=64)
-            nc.vector.quantize_mx(out=codes[:].bitcast(E5M2X4), scales=scales[:], in_=grouped[:])
+            nc.vector.quantize_mx(
+                out=codes[:, : count * P].bitcast(E5M2X4),
+                scales=scales[:, : count * P],
+                in_=grouped[:, : count * K],
+            )
             return codes, scales
 
         grouped_of = {0: transposes(0)}
-        quantised_of = {0: quantise(grouped_of[0])}
+        quantised_of = {0: quantise(0, grouped_of[0])}
 
         w_grouped = []
         for h in range(2):
@@ -103,35 +109,51 @@ def tile_lsquantlinearlayer_t_kernel(tc, inputs, weight, bias, clip_max, grad_ou
             w_scales.append(ws)
 
         grouped_of[1] = transposes(1)
+        quantised_of[1] = quantise(1, grouped_of[1])
 
-        out_sb = None
-        for q in range(N_GROUPS):
-            codes, scales = quantised_of[q]
-            for a in range(GROUP):
-                t = GROUP * q + a
-                if t % STORE_TILES == 0:
-                    out_sb = keep.tile([P, STORE_TILES * N], F32, name="out_sb%d" % t)
-                base = (t % STORE_TILES) * N
+        out_of = {}
+        for t in range(0, N_TILES, STORE_TILES):
+            out_sb = keep.tile([P, STORE_TILES * N], F32, name="out_sb%d" % t)
+            for i in range(STORE_TILES):
+                out_of[t + i] = out_sb[:, i * N : (i + 1) * N]
+            out_of[(t, "whole")] = out_sb
+
+        def product(gi, a, h):
+            codes, scales = quantised_of[gi]
+            acc = psum_o.tile([P, HALF], F32, name="acc")
+            nc.tensor.matmul_mx(
+                out=acc[:],
+                lhsT=codes[:, a * P : (a + 1) * P].bitcast(E5M2X4),
+                lhsT_scale=scales[:, a * P : (a + 1) * P],
+                rhs=w_codes[h][:].bitcast(E4M3X4),
+                rhs_scale=w_scales[h][:],
+                start=True,
+                stop=True,
+            )
+            dst = out_of[GROUPS[gi][0] + a][:, h * HALF : (h + 1) * HALF]
+            if h == 0:
+                nc.scalar.copy(out=dst, in_=acc[:])
+            else:
+                nc.vector.tensor_copy(out=dst, in_=acc[:])
+
+        def store_if_full(t):
+            if t % STORE_TILES == STORE_TILES - 1:
+                first = t - STORE_TILES + 1
+                nc.sync.dma_start(out=out_rows[:, first * N : (t + 1) * N], in_=out_of[(first, "whole")][:])
+
+        for gi, (first, count) in enumerate(GROUPS):
+            if gi == 0:
                 for h in range(2):
-                    acc = psum_o.tile([P, HALF], F32, name="acc")
-                    nc.tensor.matmul_mx(
-                        out=acc[:],
-                        lhsT=codes[:, a * P : (a + 1) * P].bitcast(E5M2X4),
-                        lhsT_scale=scales[:, a * P : (a + 1) * P],
-                        rhs=w_codes[h][:].bitcast(E4M3X4),
-                        rhs_scale=w_scales[h][:],
-                        start=True,
-                        stop=True,
-                    )
-                    dst = out_sb[:, base + h * HALF : base + (h + 1) * HALF]
-                    if h == 0:
-                        nc.scalar.copy(out=dst, in_=acc[:])
-                    else:
-                        nc.vector.tensor_copy(out=dst, in_=acc[:])
-                if t % STORE_TILES == STORE_TILES - 1:
-                    first = t - STORE_TILES + 1
-                    nc.sync.dma_start(out=out_rows[:, first * N : (t + 1) * N], in_=out_sb[:])
-                if a == 1 and q + 1 < N_GROUPS:
-                    quantised_of[q + 1] = quantise(grouped_of[q + 1])
-            if q + 2 < N_GROUPS:
-                grouped_of[q + 2] = transposes(q + 2)
+                    for a in range(count):
+                        product(gi, a, h)
+                for a in range(count):
+                    store_if_full(first + a)
+            else:
+                for a in range(count):
+                    for h in range(2):
+                        product(gi, a, h)
+                    store_if_full(first + a)
+                    if a == count // 2 - 1 and gi + 1 < len(GROUPS):
+                        quantised_of[gi + 1] = quantise(gi + 1, grouped_of[gi + 1])
+            if gi + 2 < len(GROUPS):
+                grouped_of[gi + 2] = transposes(gi + 2)

@@ -19,7 +19,7 @@ N_TILES = TOKENS // P
 GROUP = 4
 GROUPS = ((0, 2), (2, 2), (4, 4), (8, 4), (12, 4), (16, 4), (20, 4), (24, 4), (28, 4))
 LOAD_CHUNKS = ((0, 2), (2, 2), (4, 4), (8, 8), (16, 16))
-STORE_TILES = 2
+STORES = ((0, 2), (2, 2), (4, 2), (6, 2), (8, 4), (12, 4), (16, 4), (20, 4), (24, 8))
 
 FLOPS = 2 * TOKENS * K * N
 BYTES = TOKENS * K * 2 + K * N * 2 + TOKENS * N * 4
@@ -112,11 +112,12 @@ def tile_lsquantlinearlayer_t_kernel(tc, inputs, weight, bias, clip_max, grad_ou
         quantised_of[1] = quantise(1, grouped_of[1])
 
         out_of = {}
-        for t in range(0, N_TILES, STORE_TILES):
-            out_sb = keep.tile([P, STORE_TILES * N], F32, name="out_sb%d" % t)
-            for i in range(STORE_TILES):
+        store_after = {}
+        for t, count in STORES:
+            out_sb = keep.tile([P, count * N], F32, name="out_sb%d" % t)
+            for i in range(count):
                 out_of[t + i] = out_sb[:, i * N : (i + 1) * N]
-            out_of[(t, "whole")] = out_sb
+            store_after[t + count - 1] = (t, out_sb)
 
         def product(gi, a, h):
             codes, scales = quantised_of[gi]
@@ -137,9 +138,9 @@ def tile_lsquantlinearlayer_t_kernel(tc, inputs, weight, bias, clip_max, grad_ou
                 nc.vector.tensor_copy(out=dst, in_=acc[:])
 
         def store_if_full(t):
-            if t % STORE_TILES == STORE_TILES - 1:
-                first = t - STORE_TILES + 1
-                nc.sync.dma_start(out=out_rows[:, first * N : (t + 1) * N], in_=out_of[(first, "whole")][:])
+            if t in store_after:
+                first, out_sb = store_after[t]
+                nc.sync.dma_start(out=out_rows[:, first * N : (t + 1) * N], in_=out_sb[:])
 
         for gi, (first, count) in enumerate(GROUPS):
             if gi == 0:

@@ -19,7 +19,7 @@ N_TILES = TOKENS // P
 GROUP = 4
 GROUPS = ((0, 2), (2, 2), (4, 4), (8, 4), (12, 4), (16, 4), (20, 4), (24, 4), (28, 4))
 LOAD_CHUNKS = ((0, 2), (2, 2), (4, 4), (8, 8), (16, 16))
-STORES = ((0, 2), (2, 2), (4, 2), (6, 2), (8, 4), (12, 4), (16, 4), (20, 4), (24, 8))
+STORES = ((0, 2), (2, 2), (4, 2), (6, 2), (8, 4), (12, 4), (16, 4), (20, 4), (24, 4), (28, 4))
 
 FLOPS = 2 * TOKENS * K * N
 BYTES = TOKENS * K * 2 + K * N * 2 + TOKENS * N * 4
@@ -113,11 +113,11 @@ def tile_lsquantlinearlayer_t_kernel(tc, inputs, weight, bias, clip_max, grad_ou
 
         out_of = {}
         store_after = {}
-        for t, count in STORES:
+        for s, (t, count) in enumerate(STORES):
             out_sb = keep.tile([P, count * N], F32, name="out_sb%d" % t)
             for i in range(count):
                 out_of[t + i] = out_sb[:, i * N : (i + 1) * N]
-            store_after[t + count - 1] = (t, out_sb)
+            store_after[t + count - 1] = (t, out_sb, nc.sync if s % 2 == 0 else nc.gpsimd)
 
         def product(gi, a, h):
             codes, scales = quantised_of[gi]
@@ -139,8 +139,8 @@ def tile_lsquantlinearlayer_t_kernel(tc, inputs, weight, bias, clip_max, grad_ou
 
         def store_if_full(t):
             if t in store_after:
-                first, out_sb = store_after[t]
-                nc.sync.dma_start(out=out_rows[:, first * N : (t + 1) * N], in_=out_sb[:])
+                first, out_sb, queue = store_after[t]
+                queue.dma_start(out=out_rows[:, first * N : (t + 1) * N], in_=out_sb[:])
 
         for gi, (first, count) in enumerate(GROUPS):
             if gi == 0:

@@ -52,6 +52,13 @@ def tile_lsquantlinearlayer_t_kernel(tc, inputs, weight, bias, clip_max, grad_ou
         ident = keep.tile([P, P], F32, name="ident")
         make_identity(nc, ident[:])
 
+        waiting = []
+
+        def start_waiting_stores():
+            for first, t, out_sb in waiting:
+                nc.scalar.dma_start(out=out_rows[:, first * N : (t + 1) * N], in_=out_sb[:])
+            waiting.clear()
+
         def transposes(gi):
             first, count = GROUPS[gi]
             banks = []
@@ -69,6 +76,7 @@ def tile_lsquantlinearlayer_t_kernel(tc, inputs, weight, bias, clip_max, grad_ou
                     out=pairs[:, 2 * b : 2 * b + 2, :, :],
                     in_=banks[b][:].rearrange("p a u r -> p a r u"),
                 )
+                start_waiting_stores()
             return grouped
 
         def quantise(gi, grouped):
@@ -117,7 +125,7 @@ def tile_lsquantlinearlayer_t_kernel(tc, inputs, weight, bias, clip_max, grad_ou
             out_sb = keep.tile([P, count * N], F32, name="out_sb%d" % t)
             for i in range(count):
                 out_of[t + i] = out_sb[:, i * N : (i + 1) * N]
-            store_after[t + count - 1] = (t, out_sb, nc.sync if s % 2 == 0 else nc.gpsimd)
+            store_after[t + count - 1] = (t, out_sb, s % 2 == 1)
 
         def product(gi, a, h):
             codes, scales = quantised_of[gi]
@@ -134,13 +142,17 @@ def tile_lsquantlinearlayer_t_kernel(tc, inputs, weight, bias, clip_max, grad_ou
             dst = out_of[GROUPS[gi][0] + a][:, h * HALF : (h + 1) * HALF]
             if h == 0:
                 nc.scalar.copy(out=dst, in_=acc[:])
+                start_waiting_stores()
             else:
                 nc.vector.tensor_copy(out=dst, in_=acc[:])
 
         def store_if_full(t):
             if t in store_after:
-                first, out_sb, queue = store_after[t]
-                queue.dma_start(out=out_rows[:, first * N : (t + 1) * N], in_=out_sb[:])
+                first, out_sb, on_scalar = store_after[t]
+                if on_scalar:
+                    waiting.append((first, t, out_sb))
+                else:
+                    nc.sync.dma_start(out=out_rows[:, first * N : (t + 1) * N], in_=out_sb[:])
 
         for gi, (first, count) in enumerate(GROUPS):
             if gi == 0:
@@ -158,3 +170,4 @@ def tile_lsquantlinearlayer_t_kernel(tc, inputs, weight, bias, clip_max, grad_ou
                         quantised_of[gi + 1] = quantise(gi + 1, grouped_of[gi + 1])
             if gi + 2 < len(GROUPS):
                 grouped_of[gi + 2] = transposes(gi + 2)
+        start_waiting_stores()

@@ -29,7 +29,7 @@ def tile_lsquantlinearlayer_t_kernel(tc, inputs, weight, bias, clip_max, grad_ou
     nc = tc.nc
     g_rows = grad_out.flatten_outer_dims().rearrange("(p t) k -> p (t k)", t=N_TILES)
     out_rows = out.flatten_outer_dims().rearrange("(p t) i -> p (t i)", t=N_TILES)
-    w_rows = weight.rearrange("(u q e) c -> q u e c", u=2, e=2)
+    w_rows = weight.rearrange("(q t) c -> q t c", t=4)
 
     with ExitStack() as ctx:
         keep = ctx.enter_context(tc.tile_pool(name="keep", bufs=1))
@@ -47,7 +47,7 @@ def tile_lsquantlinearlayer_t_kernel(tc, inputs, weight, bias, clip_max, grad_ou
             for i in range(count):
                 g_words[first + i] = words[:, i * (K // 2) : (i + 1) * (K // 2)]
             if c == 0:
-                nc.sync.dma_start(out=w_raw[:].rearrange("p (u e) c -> p u e c", u=2), in_=w_rows)
+                nc.sync.dma_start(out=w_raw[:], in_=w_rows)
 
         ident = keep.tile([P, P], F32, name="ident")
         make_identity(nc, ident[:])
@@ -67,7 +67,7 @@ def tile_lsquantlinearlayer_t_kernel(tc, inputs, weight, bias, clip_max, grad_ou
                 for a in range(2):
                     words = g_words[first + 2 * b + a]
                     for u in range(2):
-                        nc.tensor.transpose(tp[:, a, u, :], words[:, u * P : (u + 1) * P], ident[:])
+                        nc.tensor.transpose(tp[:, a, u, :], words[:, u : K // 2 : 2], ident[:])
                 banks.append(tp)
             grouped = stage.tile([P, GROUP * K], BF16, name="grouped", align_bytes=64)
             pairs = grouped[:].bitcast(F32).rearrange("p (a r u) -> p a r u", a=GROUP, u=2)

from contextlib import ExitStack

import concourse.mybir as mybir
from concourse.masks import make_identity

F32 = mybir.dt.float32
BF16 = mybir.dt.bfloat16
U32 = mybir.dt.uint32
U8 = mybir.dt.uint8
E5M2X4 = mybir.dt.float8_e5m2_x4
E4M3X4 = mybir.dt.float8_e4m3fn_x4

P = 128
TOKENS = 4096
K = 512
N = 1024
HALF = 512
N_TILES = TOKENS // P
GROUP = 4
GROUPS = ((0, 2), (2, 2), (4, 4), (8, 4), (12, 4), (16, 4), (20, 4), (24, 4), (28, 4))
LOAD_CHUNKS = ((0, 2), (2, 2), (4, 4), (8, 8), (16, 16))
STORES = ((0, 2), (2, 2), (4, 2), (6, 2), (8, 4), (12, 4), (16, 4), (20, 4), (24, 4), (28, 4))

FLOPS = 2 * TOKENS * K * N
BYTES = TOKENS * K * 2 + K * N * 2 + TOKENS * N * 4


def tile_lsquantlinearlayer_t_kernel(tc, inputs, weight, bias, clip_max, grad_out, out):
    nc = tc.nc
    g_rows = grad_out.flatten_outer_dims().rearrange("(p t) k -> p (t k)", t=N_TILES)
    out_rows = out.flatten_outer_dims().rearrange("(p t) i -> p (t i)", t=N_TILES)
    w_rows = weight.rearrange("(q t) c -> q t c", t=4)

    with ExitStack() as ctx:
        keep = ctx.enter_context(tc.tile_pool(name="keep", bufs=1))
        stage = ctx.enter_context(tc.tile_pool(name="stage", bufs=3))
        psum_t = ctx.enter_context(tc.psum_pool(name="psum_t", bufs=2))
        psum_o = ctx.enter_context(tc.psum_pool(name="psum_o", bufs=6))
        ctx.enter_context(tc.manual_schedule())

        g_words = {}
        w_raw = keep.tile([P, 4, N], BF16, name="w_raw")
        for c, (first, count) in enumerate(LOAD_CHUNKS):
            g_sb = keep.tile([P, count * K], BF16, name="g_sb%d" % c)
            nc.sync.dma_start(out=g_sb[:], in_=g_rows[:, first * K : (first + count) * K])
            words = g_sb[:].bitcast(F32)
            for i in range(count):
                g_words[first + i] = words[:, i * (K // 2) : (i + 1) * (K // 2)]
            if c == 0:
                nc.sync.dma_start(out=w_raw[:], in_=w_rows)

        ident = keep.tile([P, P], F32, name="ident")
        make_identity(nc, ident[:])

        waiting = []

        def start_waiting_stores():
            for first, t, out_sb in waiting:
                nc.scalar.dma_start(out=out_rows[:, first * N : (t + 1) * N], in_=out_sb[:])
            waiting.clear()

        def transposes(gi):
            first, count = GROUPS[gi]
            banks = []
            for b in range(count // 2):
                tp = psum_t.tile([P, 2, 2, P], F32, name="tp")
                for a in range(2):
                    words = g_words[first + 2 * b + a]
                    for u in range(2):
                        nc.tensor.transpose(tp[:, a, u, :], words[:, u : K // 2 : 2], ident[:])
                banks.append(tp)
            grouped = stage.tile([P, GROUP * K], BF16, name="grouped", align_bytes=64)
            pairs = grouped[:].bitcast(F32).rearrange("p (a r u) -> p a r u", a=GROUP, u=2)
            for b in range(count // 2):
                nc.scalar.copy(
                    out=pairs[:, 2 * b : 2 * b + 2, :, :],
                    in_=banks[b][:].rearrange("p a u r -> p a r u"),
                )
                start_waiting_stores()
            return grouped

        def quantise(gi, grouped):
            count = GROUPS[gi][1]
            codes = stage.tile([P, GROUP * P], U32, name="g_codes", align_bytes=64)
            scales = stage.tile([P, GROUP * P], U8, name="g_scales", align_bytes=64)
            nc.vector.quantize_mx(
                out=codes[:, : count * P].bitcast(E5M2X4),
                scales=scales[:, : count * P],
                in_=grouped[:, : count * K],
            )
            return codes, scales

        grouped_of = {0: transposes(0)}
        quantised_of = {0: quantise(0, grouped_of[0])}

        w_grouped = []
        for h in range(2):
            wg = keep.tile([P, HALF, 4], BF16, name="w_grouped%d" % h, align_bytes=64)
            dst = wg[:].rearrange("p (c i) t -> p c t i", i=4)
            src = w_raw[:, :, h * HALF : (h + 1) * HALF].rearrange("p t (c i) -> p c t i", i=4)
            if h == 0:
                nc.vector.tensor_copy(out=dst, in_=src)
            else:
                nc.scalar.copy(out=dst, in_=src)
            w_grouped.append(wg)
        w_codes = []
        w_scales = []
        for h in range(2):
            wc = keep.tile([P, HALF], U32, name="w_codes%d" % h, align_bytes=64)
            ws = keep.tile([P, HALF], U8, name="w_scales%d" % h, align_bytes=64)
            nc.vector.quantize_mx(
                out=wc[:].bitcast(E4M3X4),
                scales=ws[:],
                in_=w_grouped[h][:].rearrange("p c t -> p (c t)"),
            )
            w_codes.append(wc)
            w_scales.append(ws)

        grouped_of[1] = transposes(1)
        quantised_of[1] = quantise(1, grouped_of[1])

        out_of = {}
        store_after = {}
        for s, (t, count) in enumerate(STORES):
            out_sb = keep.tile([P, count * N], F32, name="out_sb%d" % t)
            for i in range(count):
                out_of[t + i] = out_sb[:, i * N : (i + 1) * N]
            store_after[t + count - 1] = (t, out_sb, s % 2 == 1)

        def product(gi, a, h):
            codes, scales = quantised_of[gi]
            acc = psum_o.tile([P, HALF], F32, name="acc")
            nc.tensor.matmul_mx(
                out=acc[:],
                lhsT=codes[:, a * P : (a + 1) * P].bitcast(E5M2X4),
                lhsT_scale=scales[:, a * P : (a + 1) * P],
                rhs=w_codes[h][:].bitcast(E4M3X4),
                rhs_scale=w_scales[h][:],
                start=True,
                stop=True,
            )
            dst = out_of[GROUPS[gi][0] + a][:, h * HALF : (h + 1) * HALF]
            if h == 0:
                nc.scalar.copy(out=dst, in_=acc[:])
                start_waiting_stores()
            else:
                nc.vector.tensor_copy(out=dst, in_=acc[:])

        def store_if_full(t):
            if t in store_after:
                first, out_sb, on_scalar = store_after[t]
                if on_scalar:
                    waiting.append((first, t, out_sb))
                else:
                    nc.sync.dma_start(out=out_rows[:, first * N : (t + 1) * N], in_=out_sb[:])

        for gi, (first, count) in enumerate(GROUPS):
            if gi == 0:
                for h in range(2):
                    for a in range(count):
                        product(gi, a, h)
                for a in range(count):
                    store_if_full(first + a)
            else:
                for a in range(count):
                    for h in range(2):
                        product(gi, a, h)
                    store_if_full(first + a)
                    if a == count // 2 - 1 and gi + 1 < len(GROUPS):
                        quantised_of[gi + 1] = quantise(gi + 1, grouped_of[gi + 1])
            if gi + 2 < len(GROUPS):
                grouped_of[gi + 2] = transposes(gi + 2)
        start_waiting_stores()
